import numpy as np
import ml_dtypes


def mxq(x, axis, fmt="e4m3"):
    dtype, down = {"e4m3": (ml_dtypes.float8_e4m3fn, 7), "e5m2": (ml_dtypes.float8_e5m2, 14)}[fmt]
    v = np.moveaxis(np.asarray(x, np.float32).astype(ml_dtypes.bfloat16).astype(np.float64), axis, -1)
    blocks = v.reshape(v.shape[:-1] + (-1, 32))
    amax = np.abs(blocks).max(-1, keepdims=True)
    byte = np.maximum(np.where(amax > 0, np.frexp(amax)[1] - 1 + 127, 0) - down, 1)
    scale = np.exp2(byte - 127.0)
    codes = (blocks / scale).astype(np.float32).astype(dtype).astype(np.float64)
    return np.moveaxis((codes * scale).reshape(v.shape), -1, axis)


WIDE = False


def mx_kscale(k):
    if not WIDE:
        return np.ones(k)
    levels = np.array([20, -20, 10, -10, 0])
    a = np.random.permutation(np.resize(levels, k // 512 * 4)).reshape(k // 512, 4)
    idx = np.arange(k)
    return np.exp2(a[idx // 512, idx % 128 // 32])


BF16 = ml_dtypes.bfloat16


def bf(x):
    return np.asarray(x, np.float32).astype(BF16)


def f64(x):
    return np.asarray(x).astype(np.float64)


B, D, U = 512, 1024, 1024


def hard_sigmoid(v):
    return np.clip(0.2 * v + 0.5, 0.0, 1.0)


def hard_sigmoid_grad(v):
    return np.where((v > -2.5) & (v < 2.5), 0.2, 0.0)


def setup_inputs():
    s = mx_kscale(B)[:, None]
    x0 = bf(np.random.standard_normal((B, D)))
    h = bf(np.random.standard_normal((B, U)))
    k = bf(np.random.standard_normal((D, 3 * U)) * 0.64 / np.sqrt(D))
    rk = bf(np.random.standard_normal((U, 3 * U)) * 0.64 / np.sqrt(U))
    b = bf(np.random.standard_normal((2, 3 * U)) * 0.2)
    g = bf(np.random.standard_normal((B, U)) * np.exp2(np.random.randint(-12, 1, (B, 1))) * 4.0 / s)
    m_x = f64(x0) @ f64(k) + f64(b)[0]
    m_i = f64(h) @ f64(rk) + f64(b)[1]
    a_zr = m_x[:, :2 * U] + m_i[:, :2 * U]
    rec_h = m_i[:, 2 * U:]
    r = hard_sigmoid(a_zr[:, U:])
    hh = np.tanh(m_x[:, 2 * U:] + r * rec_h)
    return {"inputs": bf(f64(x0) * s), "h_tm1": h, "kernel": k, "recurrent_kernel": rk, "bias": b,
            "a_zr": np.asarray(a_zr, np.float32), "rec_h": np.asarray(rec_h, np.float32),
            "hh": np.asarray(hh, np.float32), "grad_out": g}


def reference(inputs, h_tm1, kernel, recurrent_kernel, bias, a_zr, rec_h, hh, grad_out):
    g = f64(grad_out)
    a = f64(a_zr)
    a_z, a_r = a[:, :U], a[:, U:]
    hhf = f64(hh)
    z = hard_sigmoid(a_z)
    d_ah = g * (1.0 - z) * (1.0 - hhf * hhf)
    d_az = g * (f64(h_tm1) - hhf) * hard_sigmoid_grad(a_z)
    d_ar = d_ah * f64(rec_h) * hard_sigmoid_grad(a_r)
    dm = np.concatenate([d_az, d_ar, d_ah], axis=1)
    return mxq(f64(inputs), 0, "e4m3").T @ mxq(dm, 0, "e5m2")

@@ -1,0 +1,217 @@
+import concourse.mybir as mybir
+
+F32 = mybir.dt.float32
+BF16 = mybir.dt.bfloat16
+U32 = mybir.dt.uint32
+U8 = mybir.dt.uint8
+E4M3X4 = mybir.dt.float8_e4m3fn_x4
+E5M2X4 = mybir.dt.float8_e5m2_x4
+ALU = mybir.AluOpType
+ACT = mybir.ActivationFunctionType
+
+P = 128
+PACK = 4
+TOKENS = P * PACK
+D = 1024
+U = 1024
+M_TILE = 128
+N_TILE = 512
+M_TILES = D // M_TILE
+HALVES = U // N_TILE
+PIECE = N_TILE // 2
+HS_SLOPE = 0.2
+HS_EDGE = 2.5
+
+FLOPS = 2 * TOKENS * D * 3 * U
+BYTES = 2 * TOKENS * (D + 2 * U) + 4 * TOKENS * 4 * U + 4 * D * 3 * U
+
+
+def tile_gruskipcell_v_kernel(
+    tc, inputs, h_tm1, kernel, recurrent_kernel, bias, a_zr, rec_h, hh, grad_out, out
+):
+    nc = tc.nc
+
+    def by_partition(dram):
+        return dram.rearrange("(p j) w -> p j w", j=PACK)
+
+    def token_last(tile_ap):
+        return tile_ap.rearrange("p j w -> p w j")
+
+    row_pairs = [slice(0, 2), slice(2, 4)]
+    col_halves = [slice(c * N_TILE, (c + 1) * N_TILE) for c in range(HALVES)]
+    pieces = [slice(k * PIECE, (k + 1) * PIECE) for k in range(N_TILE // PIECE)]
+
+    def pieces_of_half(c):
+        return [
+            (pieces[k], slice(c * N_TILE + k * PIECE, c * N_TILE + (k + 1) * PIECE))
+            for k in range(N_TILE // PIECE)
+        ]
+
+    with tc.tile_pool(name="resident", bufs=1) as resident, tc.tile_pool(
+        name="grouped", bufs=3
+    ) as grouped_pool, tc.tile_pool(name="quantised", bufs=3) as quantised, tc.tile_pool(
+        name="staging", bufs=16
+    ) as staging, tc.psum_pool(name="banks", bufs=8) as banks, tc.manual_schedule():
+        x_sb = resident.tile([P, PACK, D], BF16)
+        g_sb = resident.tile([P, PACK, U], BF16)
+        h_sb = resident.tile([P, PACK, U], BF16)
+        az_sb = resident.tile([P, PACK, U], F32)
+        hh_sb = resident.tile([P, PACK, U], F32)
+        ar_sb = resident.tile([P, PACK, U], F32)
+        rh_sb = resident.tile([P, PACK, U], F32)
+        u5_sb = resident.tile([P, PACK, U], F32)
+        t_sb = resident.tile([P, PACK, U], F32)
+        sq_sb = resident.tile([P, PACK, U], F32)
+        x_grouped = resident.tile([P, D, PACK], BF16, align_bytes=64)
+        x_codes = resident.tile([P, D], U32, align_bytes=64)
+        x_scales = resident.tile([P, D], U8, align_bytes=64)
+        q5_sb = [
+            resident.tile([P, N_TILE, PACK], F32, name="q5_%d" % c) for c in range(HALVES)
+        ]
+
+        nc.sync.dma_start(out=x_sb[:], in_=by_partition(inputs))
+        for rows in row_pairs:
+            nc.sync.dma_start(out=az_sb[:, rows, :], in_=by_partition(a_zr)[:, rows, 0:U])
+        nc.sync.dma_start(out=g_sb[:], in_=by_partition(grad_out))
+        nc.sync.dma_start(out=h_sb[:], in_=by_partition(h_tm1))
+        for rows in row_pairs:
+            nc.sync.dma_start(out=hh_sb[:, rows, :], in_=by_partition(hh)[:, rows, :])
+        for rows in row_pairs:
+            nc.sync.dma_start(out=ar_sb[:, rows, :], in_=by_partition(a_zr)[:, rows, U : 2 * U])
+        for rows in row_pairs:
+            nc.sync.dma_start(out=rh_sb[:, rows, :], in_=by_partition(rec_h)[:, rows, :])
+
+        def quantise_multiply_store(grouped, first_column, vector_helps):
+            dm_codes = quantised.tile([P, N_TILE], U32, align_bytes=64)
+            dm_scales = quantised.tile([P, N_TILE], U8, align_bytes=64)
+            for piece in pieces:
+                nc.vector.quantize_mx(
+                    out=dm_codes[:, piece].bitcast(E5M2X4),
+                    scales=dm_scales[:, piece],
+                    in_=grouped[:, piece, :].rearrange("p w j -> p (w j)"),
+                )
+            for m in range(M_TILES):
+                m_cols = slice(m * M_TILE, (m + 1) * M_TILE)
+                acc = banks.tile([P, N_TILE], F32)
+                nc.tensor.matmul_mx(
+                    out=acc[:],
+                    lhsT=x_codes[:, m_cols].bitcast(E4M3X4),
+                    lhsT_scale=x_scales[:, m_cols],
+                    rhs=dm_codes[:].bitcast(E5M2X4),
+                    rhs_scale=dm_scales[:],
+                    start=True,
+                    stop=True,
+                )
+                staged = staging.tile([P, N_TILE], F32)
+                if vector_helps and m < M_TILES // 2:
+                    nc.vector.tensor_copy(out=staged[:], in_=acc[:])
+                else:
+                    nc.scalar.copy(out=staged[:], in_=acc[:])
+                nc.sync.dma_start(
+                    out=out[m_cols, first_column : first_column + N_TILE], in_=staged[:]
+                )
+
+        for cols in col_halves:
+            nc.vector.tensor_copy(
+                out=x_grouped[:, cols, :].rearrange("p (c i) j -> p c j i", i=4),
+                in_=x_sb[:, :, cols].rearrange("p j (c i) -> p c j i", i=4),
+            )
+        for cols in col_halves:
+            nc.vector.quantize_mx(
+                out=x_codes[:, cols].bitcast(E4M3X4),
+                scales=x_scales[:, cols],
+                in_=x_grouped[:, cols, :].rearrange("p w j -> p (w j)"),
+            )
+
+        for rows in row_pairs:
+            nc.vector.tensor_scalar(
+                out=u5_sb[:, rows, :],
+                in0=az_sb[:, rows, :],
+                scalar1=-HS_EDGE,
+                scalar2=HS_EDGE,
+                op0=ALU.max,
+                op1=ALU.min,
+            )
+        for rows in row_pairs:
+            nc.scalar.activation(out=az_sb[:, rows, :], in_=az_sb[:, rows, :], func=ACT.Abs)
+        for rows in row_pairs:
+            nc.vector.scalar_tensor_tensor(
+                out=u5_sb[:, rows, :],
+                in0=u5_sb[:, rows, :],
+                scalar=HS_EDGE,
+                in1=g_sb[:, rows, :],
+                op0=ALU.subtract,
+                op1=ALU.mult,
+            )
+        for rows in row_pairs:
+            nc.vector.tensor_tensor(
+                out=t_sb[:, rows, :], in0=h_sb[:, rows, :], in1=hh_sb[:, rows, :], op=ALU.subtract
+            )
+            nc.scalar.activation(out=sq_sb[:, rows, :], in_=hh_sb[:, rows, :], func=ACT.Square)
+        for rows in row_pairs:
+            nc.scalar.activation(out=ar_sb[:, rows, :], in_=ar_sb[:, rows, :], func=ACT.Abs)
+
+        for c in range(HALVES):
+            for piece, cols in pieces_of_half(c):
+                nc.vector.scalar_tensor_tensor(
+                    out=q5_sb[c][:, piece, :],
+                    in0=token_last(sq_sb[:, :, cols]),
+                    scalar=1.0,
+                    in1=token_last(u5_sb[:, :, cols]),
+                    op0=ALU.subtract,
+                    op1=ALU.mult,
+                )
+            d_ah = grouped_pool.tile([P, N_TILE, PACK], BF16, tag="grouped", align_bytes=64)
+            for piece in pieces:
+                nc.vector.tensor_scalar(
+                    out=d_ah[:, piece, :],
+                    in0=q5_sb[c][:, piece, :],
+                    scalar1=HS_SLOPE,
+                    scalar2=None,
+                    op0=ALU.mult,
+                )
+            quantise_multiply_store(d_ah, 2 * U + c * N_TILE, False)
+
+        for cols in col_halves:
+            nc.vector.scalar_tensor_tensor(
+                out=t_sb[:, :, cols],
+                in0=az_sb[:, :, cols],
+                scalar=HS_EDGE,
+                in1=t_sb[:, :, cols],
+                op0=ALU.is_lt,
+                op1=ALU.mult,
+            )
+        for c in range(HALVES):
+            d_az = grouped_pool.tile([P, N_TILE, PACK], BF16, tag="grouped", align_bytes=64)
+            for piece, cols in pieces_of_half(c):
+                nc.vector.scalar_tensor_tensor(
+                    out=d_az[:, piece, :],
+                    in0=token_last(t_sb[:, :, cols]),
+                    scalar=HS_SLOPE,
+                    in1=token_last(g_sb[:, :, cols]),
+                    op0=ALU.mult,
+                    op1=ALU.mult,
+                )
+            quantise_multiply_store(d_az, c * N_TILE, False)
+
+        for cols in col_halves:
+            nc.vector.scalar_tensor_tensor(
+                out=rh_sb[:, :, cols],
+                in0=ar_sb[:, :, cols],
+                scalar=HS_EDGE,
+                in1=rh_sb[:, :, cols],
+                op0=ALU.is_lt,
+                op1=ALU.mult,
+            )
+        for c in range(HALVES):
+            d_ar = grouped_pool.tile([P, N_TILE, PACK], BF16, tag="grouped", align_bytes=64)
+            for piece, cols in pieces_of_half(c):
+                nc.vector.scalar_tensor_tensor(
+                    out=d_ar[:, piece, :],
+                    in0=token_last(rh_sb[:, :, cols]),
+                    scalar=HS_SLOPE * HS_SLOPE,
+                    in1=q5_sb[c][:, piece, :],
+                    op0=ALU.mult,
+                    op1=ALU.mult,
+                )
+            quantise_multiply_store(d_ar, U + c * N_TILE, c == HALVES - 1)

@@ -172,16 +172,16 @@ def tile_gruskipcell_v_kernel(
                 )
             quantise_multiply_store(d_ah, 2 * U + c * N_TILE, False)
 
-        for cols in col_halves:
-            nc.vector.scalar_tensor_tensor(
-                out=t_sb[:, :, cols],
-                in0=az_sb[:, :, cols],
-                scalar=HS_EDGE,
-                in1=t_sb[:, :, cols],
-                op0=ALU.is_lt,
-                op1=ALU.mult,
-            )
         for c in range(HALVES):
+            for piece, cols in pieces_of_half(c):
+                nc.vector.scalar_tensor_tensor(
+                    out=t_sb[:, :, cols],
+                    in0=az_sb[:, :, cols],
+                    scalar=HS_EDGE,
+                    in1=t_sb[:, :, cols],
+                    op0=ALU.is_lt,
+                    op1=ALU.mult,
+                )
             d_az = grouped_pool.tile([P, N_TILE, PACK], BF16, tag="grouped", align_bytes=64)
             for piece, cols in pieces_of_half(c):
                 nc.vector.scalar_tensor_tensor(
@@ -194,16 +194,16 @@ def tile_gruskipcell_v_kernel(
                 )
             quantise_multiply_store(d_az, c * N_TILE, False)
 
-        for cols in col_halves:
-            nc.vector.scalar_tensor_tensor(
-                out=rh_sb[:, :, cols],
-                in0=ar_sb[:, :, cols],
-                scalar=HS_EDGE,
-                in1=rh_sb[:, :, cols],
-                op0=ALU.is_lt,
-                op1=ALU.mult,
-            )
         for c in range(HALVES):
+            for piece, cols in pieces_of_half(c):
+                nc.vector.scalar_tensor_tensor(
+                    out=rh_sb[:, :, cols],
+                    in0=ar_sb[:, :, cols],
+                    scalar=HS_EDGE,
+                    in1=rh_sb[:, :, cols],
+                    op0=ALU.is_lt,
+                    op1=ALU.mult,
+                )
             d_ar = grouped_pool.tile([P, N_TILE, PACK], BF16, tag="grouped", align_bytes=64)
             for piece, cols in pieces_of_half(c):
                 nc.vector.scalar_tensor_tensor(

@@ -69,17 +69,15 @@ def tile_gruskipcell_v_kernel(
             resident.tile([P, N_TILE, PACK], F32, name="q5_%d" % c) for c in range(HALVES)
         ]
 
-        nc.sync.dma_start(out=x_sb[:], in_=by_partition(inputs))
-        for rows in row_pairs:
-            nc.sync.dma_start(out=az_sb[:, rows, :], in_=by_partition(a_zr)[:, rows, 0:U])
+        nc.sync.dma_start(out=az_sb[:, row_pairs[0], :], in_=by_partition(a_zr)[:, row_pairs[0], 0:U])
         nc.sync.dma_start(out=g_sb[:], in_=by_partition(grad_out))
+        nc.sync.dma_start(out=az_sb[:, row_pairs[1], :], in_=by_partition(a_zr)[:, row_pairs[1], 0:U])
         nc.sync.dma_start(out=h_sb[:], in_=by_partition(h_tm1))
         for rows in row_pairs:
             nc.sync.dma_start(out=hh_sb[:, rows, :], in_=by_partition(hh)[:, rows, :])
-        for rows in row_pairs:
-            nc.sync.dma_start(out=ar_sb[:, rows, :], in_=by_partition(a_zr)[:, rows, U : 2 * U])
-        for rows in row_pairs:
-            nc.sync.dma_start(out=rh_sb[:, rows, :], in_=by_partition(rec_h)[:, rows, :])
+        nc.sync.dma_start(out=x_sb[:], in_=by_partition(inputs))
+        nc.sync.dma_start(out=ar_sb[:], in_=by_partition(a_zr)[:, :, U : 2 * U])
+        nc.sync.dma_start(out=rh_sb[:], in_=by_partition(rec_h))
 
         def quantise_multiply_store(grouped, first_column, vector_helps):
             dm_codes = quantised.tile([P, N_TILE], U32, align_bytes=64)
@@ -103,25 +101,13 @@ def tile_gruskipcell_v_kernel(
                     stop=True,
                 )
                 staged = staging.tile([P, N_TILE], F32)
-                if vector_helps and m < M_TILES // 2:
+                if vector_helps and m % 2 == 0:
                     nc.vector.tensor_copy(out=staged[:], in_=acc[:])
                 else:
                     nc.scalar.copy(out=staged[:], in_=acc[:])
                 nc.sync.dma_start(
                     out=out[m_cols, first_column : first_column + N_TILE], in_=staged[:]
                 )
-
-        for cols in col_halves:
-            nc.vector.tensor_copy(
-                out=x_grouped[:, cols, :].rearrange("p (c i) j -> p c j i", i=4),
-                in_=x_sb[:, :, cols].rearrange("p j (c i) -> p c j i", i=4),
-            )
-        for cols in col_halves:
-            nc.vector.quantize_mx(
-                out=x_codes[:, cols].bitcast(E4M3X4),
-                scales=x_scales[:, cols],
-                in_=x_grouped[:, cols, :].rearrange("p w j -> p (w j)"),
-            )
 
         for rows in row_pairs:
             nc.vector.tensor_scalar(
@@ -132,9 +118,7 @@ def tile_gruskipcell_v_kernel(
                 op0=ALU.max,
                 op1=ALU.min,
             )
-        for rows in row_pairs:
             nc.scalar.activation(out=az_sb[:, rows, :], in_=az_sb[:, rows, :], func=ACT.Abs)
-        for rows in row_pairs:
             nc.vector.scalar_tensor_tensor(
                 out=u5_sb[:, rows, :],
                 in0=u5_sb[:, rows, :],
@@ -148,6 +132,11 @@ def tile_gruskipcell_v_kernel(
                 out=t_sb[:, rows, :], in0=h_sb[:, rows, :], in1=hh_sb[:, rows, :], op=ALU.subtract
             )
             nc.scalar.activation(out=sq_sb[:, rows, :], in_=hh_sb[:, rows, :], func=ACT.Square)
+        for cols in col_halves:
+            nc.scalar.copy(
+                out=x_grouped[:, cols, :].rearrange("p (c i) j -> p c j i", i=4),
+                in_=x_sb[:, :, cols].rearrange("p j (c i) -> p c j i", i=4),
+            )
         for rows in row_pairs:
             nc.scalar.activation(out=ar_sb[:, rows, :], in_=ar_sb[:, rows, :], func=ACT.Abs)
 
@@ -170,6 +159,13 @@ def tile_gruskipcell_v_kernel(
                     scalar2=None,
                     op0=ALU.mult,
                 )
+            if c == 0:
+                for cols in col_halves:
+                    nc.vector.quantize_mx(
+                        out=x_codes[:, cols].bitcast(E4M3X4),
+                        scales=x_scales[:, cols],
+                        in_=x_grouped[:, cols, :].rearrange("p w j -> p (w j)"),
+                    )
             quantise_multiply_store(d_ah, 2 * U + c * N_TILE, False)
 
         for c in range(HALVES):

@@ -37,6 +37,7 @@ def tile_gruskipcell_v_kernel(
     def token_last(tile_ap):
         return tile_ap.rearrange("p j w -> p w j")
 
+    rows_of = [slice(j, j + 1) for j in range(PACK)]
     row_pairs = [slice(0, 2), slice(2, 4)]
     col_halves = [slice(c * N_TILE, (c + 1) * N_TILE) for c in range(HALVES)]
     pieces = [slice(k * PIECE, (k + 1) * PIECE) for k in range(N_TILE // PIECE)]
@@ -59,27 +60,21 @@ def tile_gruskipcell_v_kernel(
         hh_sb = resident.tile([P, PACK, U], F32)
         ar_sb = resident.tile([P, PACK, U], F32)
         rh_sb = resident.tile([P, PACK, U], F32)
-        u5_sb = resident.tile([P, PACK, U], F32)
+        q5_sb = resident.tile([P, PACK, U], F32)
+        gm_sb = resident.tile([P, PACK, U], BF16)
         t_sb = resident.tile([P, PACK, U], F32)
         sq_sb = resident.tile([P, PACK, U], F32)
         x_grouped = resident.tile([P, D, PACK], BF16, align_bytes=64)
         x_codes = resident.tile([P, D], U32, align_bytes=64)
         x_scales = resident.tile([P, D], U8, align_bytes=64)
-        q5_sb = [
-            resident.tile([P, N_TILE, PACK], F32, name="q5_%d" % c) for c in range(HALVES)
-        ]
 
-        nc.sync.dma_start(out=az_sb[:, row_pairs[0], :], in_=by_partition(a_zr)[:, row_pairs[0], 0:U])
-        nc.sync.dma_start(out=g_sb[:], in_=by_partition(grad_out))
-        nc.sync.dma_start(out=az_sb[:, row_pairs[1], :], in_=by_partition(a_zr)[:, row_pairs[1], 0:U])
-        nc.sync.dma_start(out=h_sb[:], in_=by_partition(h_tm1))
-        for rows in row_pairs:
-            nc.sync.dma_start(out=hh_sb[:, rows, :], in_=by_partition(hh)[:, rows, :])
-        nc.sync.dma_start(out=x_sb[:], in_=by_partition(inputs))
-        nc.sync.dma_start(out=ar_sb[:], in_=by_partition(a_zr)[:, :, U : 2 * U])
-        nc.sync.dma_start(out=rh_sb[:], in_=by_partition(rec_h))
+        def load(tile, dram, rows, cols=None):
+            if cols is None:
+                nc.sync.dma_start(out=tile[:, rows, :], in_=by_partition(dram)[:, rows, :])
+            else:
+                nc.sync.dma_start(out=tile[:, rows, :], in_=by_partition(dram)[:, rows, cols])
 
-        def quantise_multiply_store(grouped, first_column, vector_helps):
+        def quantise(grouped):
             dm_codes = quantised.tile([P, N_TILE], U32, align_bytes=64)
             dm_scales = quantised.tile([P, N_TILE], U8, align_bytes=64)
             for piece in pieces:
@@ -88,7 +83,11 @@ def tile_gruskipcell_v_kernel(
                     scales=dm_scales[:, piece],
                     in_=grouped[:, piece, :].rearrange("p w j -> p (w j)"),
                 )
-            for m in range(M_TILES):
+            return dm_codes, dm_scales
+
+        def passes(codes, first_column, ms, vector_ms=()):
+            dm_codes, dm_scales = codes
+            for m in ms:
                 m_cols = slice(m * M_TILE, (m + 1) * M_TILE)
                 acc = banks.tile([P, N_TILE], F32)
                 nc.tensor.matmul_mx(
@@ -101,96 +100,112 @@ def tile_gruskipcell_v_kernel(
                     stop=True,
                 )
                 staged = staging.tile([P, N_TILE], F32)
-                if vector_helps and m % 2 == 0:
+                if m in vector_ms:
                     nc.vector.tensor_copy(out=staged[:], in_=acc[:])
                 else:
                     nc.scalar.copy(out=staged[:], in_=acc[:])
-                nc.sync.dma_start(
-                    out=out[m_cols, first_column : first_column + N_TILE], in_=staged[:]
-                )
+                nc.sync.dma_start(out=out[m_cols, first_column : first_column + N_TILE], in_=staged[:])
 
-        for rows in row_pairs:
+        def clip_az(rows):
             nc.vector.tensor_scalar(
-                out=u5_sb[:, rows, :],
+                out=q5_sb[:, rows, :],
                 in0=az_sb[:, rows, :],
                 scalar1=-HS_EDGE,
                 scalar2=HS_EDGE,
                 op0=ALU.max,
                 op1=ALU.min,
             )
+
+        def abs_az(rows):
             nc.scalar.activation(out=az_sb[:, rows, :], in_=az_sb[:, rows, :], func=ACT.Abs)
+
+        def times_grad(rows):
             nc.vector.scalar_tensor_tensor(
-                out=u5_sb[:, rows, :],
-                in0=u5_sb[:, rows, :],
+                out=q5_sb[:, rows, :],
+                in0=q5_sb[:, rows, :],
                 scalar=HS_EDGE,
                 in1=g_sb[:, rows, :],
                 op0=ALU.subtract,
                 op1=ALU.mult,
             )
-        for rows in row_pairs:
-            nc.vector.tensor_tensor(
-                out=t_sb[:, rows, :], in0=h_sb[:, rows, :], in1=hh_sb[:, rows, :], op=ALU.subtract
+
+        def masked_grad(rows):
+            nc.vector.scalar_tensor_tensor(
+                out=gm_sb[:, rows, :],
+                in0=az_sb[:, rows, :],
+                scalar=HS_EDGE,
+                in1=g_sb[:, rows, :],
+                op0=ALU.is_lt,
+                op1=ALU.mult,
             )
+
+        def square_hh(rows):
             nc.scalar.activation(out=sq_sb[:, rows, :], in_=hh_sb[:, rows, :], func=ACT.Square)
-        for cols in col_halves:
+
+        def difference(rows, cols):
+            nc.vector.tensor_tensor(
+                out=t_sb[:, rows, cols], in0=h_sb[:, rows, cols], in1=hh_sb[:, rows, cols], op=ALU.subtract
+            )
+
+        def regroup_x(c):
+            cols = col_halves[c]
             nc.scalar.copy(
                 out=x_grouped[:, cols, :].rearrange("p (c i) j -> p c j i", i=4),
                 in_=x_sb[:, :, cols].rearrange("p j (c i) -> p c j i", i=4),
             )
-        for rows in row_pairs:
-            nc.scalar.activation(out=ar_sb[:, rows, :], in_=ar_sb[:, rows, :], func=ACT.Abs)
 
-        for c in range(HALVES):
-            for piece, cols in pieces_of_half(c):
+        def quantise_x(c):
+            cols = col_halves[c]
+            nc.vector.quantize_mx(
+                out=x_codes[:, cols].bitcast(E4M3X4),
+                scales=x_scales[:, cols],
+                in_=x_grouped[:, cols, :].rearrange("p w j -> p (w j)"),
+            )
+
+        def times_one_minus_square(rows):
+            for cols in col_halves:
                 nc.vector.scalar_tensor_tensor(
-                    out=q5_sb[c][:, piece, :],
-                    in0=token_last(sq_sb[:, :, cols]),
+                    out=q5_sb[:, rows, cols],
+                    in0=sq_sb[:, rows, cols],
                     scalar=1.0,
-                    in1=token_last(u5_sb[:, :, cols]),
+                    in1=q5_sb[:, rows, cols],
                     op0=ALU.subtract,
                     op1=ALU.mult,
                 )
-            d_ah = grouped_pool.tile([P, N_TILE, PACK], BF16, tag="grouped", align_bytes=64)
-            for piece in pieces:
+
+        def new_grouped():
+            grouped = grouped_pool.tile([P, N_TILE, PACK], BF16, tag="grouped", align_bytes=64)
+            return grouped
+
+        def round_ah(c):
+            d_ah = new_grouped()
+            for piece, cols in pieces_of_half(c):
                 nc.vector.tensor_scalar(
                     out=d_ah[:, piece, :],
-                    in0=q5_sb[c][:, piece, :],
+                    in0=token_last(q5_sb[:, :, cols]),
                     scalar1=HS_SLOPE,
                     scalar2=None,
                     op0=ALU.mult,
                 )
-            if c == 0:
-                for cols in col_halves:
-                    nc.vector.quantize_mx(
-                        out=x_codes[:, cols].bitcast(E4M3X4),
-                        scales=x_scales[:, cols],
-                        in_=x_grouped[:, cols, :].rearrange("p w j -> p (w j)"),
-                    )
-            quantise_multiply_store(d_ah, 2 * U + c * N_TILE, False)
+            return d_ah
 
-        for c in range(HALVES):
-            for piece, cols in pieces_of_half(c):
-                nc.vector.scalar_tensor_tensor(
-                    out=t_sb[:, :, cols],
-                    in0=az_sb[:, :, cols],
-                    scalar=HS_EDGE,
-                    in1=t_sb[:, :, cols],
-                    op0=ALU.is_lt,
-                    op1=ALU.mult,
-                )
-            d_az = grouped_pool.tile([P, N_TILE, PACK], BF16, tag="grouped", align_bytes=64)
+        def abs_ar(rows, cols):
+            nc.scalar.activation(out=ar_sb[:, rows, cols], in_=ar_sb[:, rows, cols], func=ACT.Abs)
+
+        def product_az(c):
+            d_az = new_grouped()
             for piece, cols in pieces_of_half(c):
                 nc.vector.scalar_tensor_tensor(
                     out=d_az[:, piece, :],
                     in0=token_last(t_sb[:, :, cols]),
                     scalar=HS_SLOPE,
-                    in1=token_last(g_sb[:, :, cols]),
+                    in1=token_last(gm_sb[:, :, cols]),
                     op0=ALU.mult,
                     op1=ALU.mult,
                 )
-            quantise_multiply_store(d_az, c * N_TILE, False)
+            return d_az
 
-        for c in range(HALVES):
+        def masked_rec(c):
             for piece, cols in pieces_of_half(c):
                 nc.vector.scalar_tensor_tensor(
                     out=rh_sb[:, :, cols],
@@ -200,14 +215,74 @@ def tile_gruskipcell_v_kernel(
                     op0=ALU.is_lt,
                     op1=ALU.mult,
                 )
-            d_ar = grouped_pool.tile([P, N_TILE, PACK], BF16, tag="grouped", align_bytes=64)
+
+        def product_ar(c):
+            d_ar = new_grouped()
             for piece, cols in pieces_of_half(c):
                 nc.vector.scalar_tensor_tensor(
                     out=d_ar[:, piece, :],
                     in0=token_last(rh_sb[:, :, cols]),
                     scalar=HS_SLOPE * HS_SLOPE,
-                    in1=q5_sb[c][:, piece, :],
+                    in1=token_last(q5_sb[:, :, cols]),
                     op0=ALU.mult,
                     op1=ALU.mult,
                 )
-            quantise_multiply_store(d_ar, U + c * N_TILE, c == HALVES - 1)
+            return d_ar
+
+        AH, AZ, AR = 2 * U, 0, U
+        ALL = slice(0, PACK)
+        Z_COLS, R_COLS = slice(0, U), slice(U, 2 * U)
+
+        load(az_sb, a_zr, rows_of[0], Z_COLS)
+        load(g_sb, grad_out, row_pairs[0])
+        load(az_sb, a_zr, rows_of[1], Z_COLS)
+        load(az_sb, a_zr, rows_of[2], Z_COLS)
+        load(g_sb, grad_out, row_pairs[1])
+        load(az_sb, a_zr, rows_of[3], Z_COLS)
+        load(hh_sb, hh, row_pairs[0])
+        load(hh_sb, hh, row_pairs[1])
+        load(x_sb, inputs, ALL)
+        load(h_sb, h_tm1, ALL)
+        load(ar_sb, a_zr, ALL, R_COLS)
+        load(rh_sb, rec_h, ALL)
+
+        for j in range(PACK):
+            clip_az(rows_of[j])
+            abs_az(rows_of[j])
+            times_grad(rows_of[j])
+        masked_grad(row_pairs[0])
+        square_hh(row_pairs[0])
+        square_hh(row_pairs[1])
+        regroup_x(0)
+        regroup_x(1)
+        times_one_minus_square(row_pairs[0])
+        times_one_minus_square(row_pairs[1])
+        quantise_x(0)
+        d_ah0 = round_ah(0)
+        a_codes = quantise(d_ah0)
+        passes(a_codes, AH, (0, 1, 2, 3))
+        d_ah1 = round_ah(1)
+        quantise_x(1)
+        b_codes = quantise(d_ah1)
+        passes(a_codes, AH, (4, 5, 6, 7))
+        abs_ar(ALL, col_halves[0])
+        masked_grad(row_pairs[1])
+        difference(ALL, col_halves[0])
+        passes(b_codes, AH + N_TILE, (0, 1, 2, 3, 4, 5, 6, 7), ())
+        d_az0 = product_az(0)
+        difference(ALL, col_halves[1])
+        c_codes = quantise(d_az0)
+        abs_ar(ALL, col_halves[1])
+        d_az1 = product_az(1)
+        passes(c_codes, AZ, (0, 1, 2, 3, 4, 5, 6, 7), ())
+        masked_rec(0)
+        d_codes = quantise(d_az1)
+        masked_rec(1)
+        d_ar0 = product_ar(0)
+        passes(d_codes, AZ + N_TILE, (0, 1, 2, 3, 4, 5, 6, 7), ())
+        e_codes = quantise(d_ar0)
+        d_ar1 = product_ar(1)
+        passes(e_codes, AR, (0, 1, 2, 3))
+        f_codes = quantise(d_ar1)
+        passes(e_codes, AR, (4, 5, 6, 7), (5, 7))
+        passes(f_codes, AR + N_TILE, (0, 1, 2, 3, 4, 5, 6, 7), (1, 3, 5, 7))

@@ -117,7 +117,7 @@ def tile_gruskipcell_v_kernel(
             )
 
         def abs_az(rows):
-            nc.scalar.activation(out=az_sb[:, rows, :], in_=az_sb[:, rows, :], func=ACT.Abs)
+            nc.scalar.activation(out=t_sb[:, rows, :], in_=az_sb[:, rows, :], func=ACT.Abs)
 
         def times_grad(rows):
             nc.vector.scalar_tensor_tensor(
@@ -132,7 +132,7 @@ def tile_gruskipcell_v_kernel(
         def masked_grad(rows):
             nc.vector.scalar_tensor_tensor(
                 out=gm_sb[:, rows, :],
-                in0=az_sb[:, rows, :],
+                in0=t_sb[:, rows, :],
                 scalar=HS_EDGE,
                 in1=g_sb[:, rows, :],
                 op0=ALU.is_lt,
@@ -247,10 +247,17 @@ def tile_gruskipcell_v_kernel(
         load(rh_sb, rec_h, ALL)
 
         for j in range(PACK):
-            clip_az(rows_of[j])
             abs_az(rows_of[j])
-            times_grad(rows_of[j])
-        masked_grad(row_pairs[0])
+        clip_az(rows_of[0])
+        times_grad(rows_of[0])
+        clip_az(rows_of[1])
+        clip_az(rows_of[2])
+        times_grad(rows_of[1])
+        times_grad(rows_of[2])
+        clip_az(rows_of[3])
+        masked_grad(rows_of[0])
+        times_grad(rows_of[3])
+        masked_grad(rows_of[1])
         square_hh(row_pairs[0])
         square_hh(row_pairs[1])
         regroup_x(0)
@@ -267,19 +274,20 @@ def tile_gruskipcell_v_kernel(
         passes(a_codes, AH, (4, 5, 6, 7))
         abs_ar(ALL, col_halves[0])
         masked_grad(row_pairs[1])
-        difference(ALL, col_halves[0])
-        passes(b_codes, AH + N_TILE, (0, 1, 2, 3, 4, 5, 6, 7), ())
+        for piece, cols in pieces_of_half(0):
+            difference(ALL, cols)
+        passes(b_codes, AH + N_TILE, (0, 1, 2, 3, 4, 5, 6, 7))
         d_az0 = product_az(0)
         difference(ALL, col_halves[1])
         c_codes = quantise(d_az0)
         abs_ar(ALL, col_halves[1])
         d_az1 = product_az(1)
-        passes(c_codes, AZ, (0, 1, 2, 3, 4, 5, 6, 7), ())
+        passes(c_codes, AZ, (0, 1, 2, 3, 4, 5, 6, 7))
         masked_rec(0)
         d_codes = quantise(d_az1)
         masked_rec(1)
         d_ar0 = product_ar(0)
-        passes(d_codes, AZ + N_TILE, (0, 1, 2, 3, 4, 5, 6, 7), ())
+        passes(d_codes, AZ + N_TILE, (0, 1, 2, 3, 4, 5, 6, 7))
         e_codes = quantise(d_ar0)
         d_ar1 = product_ar(1)
         passes(e_codes, AR, (0, 1, 2, 3))

@@ -68,11 +68,13 @@ def tile_gruskipcell_v_kernel(
         x_codes = resident.tile([P, D], U32, align_bytes=64)
         x_scales = resident.tile([P, D], U8, align_bytes=64)
 
-        def load(tile, dram, rows, cols=None):
+        def load(tile, dram, rows, cols=None, to_cols=None):
             if cols is None:
                 nc.sync.dma_start(out=tile[:, rows, :], in_=by_partition(dram)[:, rows, :])
-            else:
+            elif to_cols is None:
                 nc.sync.dma_start(out=tile[:, rows, :], in_=by_partition(dram)[:, rows, cols])
+            else:
+                nc.sync.dma_start(out=tile[:, rows, to_cols], in_=by_partition(dram)[:, rows, cols])
 
         def quantise(grouped):
             dm_codes = quantised.tile([P, N_TILE], U32, align_bytes=64)
@@ -106,25 +108,25 @@ def tile_gruskipcell_v_kernel(
                     nc.scalar.copy(out=staged[:], in_=acc[:])
                 nc.sync.dma_start(out=out[m_cols, first_column : first_column + N_TILE], in_=staged[:])
 
-        def clip_az(rows):
+        def clip_az(rows, cols=slice(0, U)):
             nc.vector.tensor_scalar(
-                out=q5_sb[:, rows, :],
-                in0=az_sb[:, rows, :],
+                out=q5_sb[:, rows, cols],
+                in0=az_sb[:, rows, cols],
                 scalar1=-HS_EDGE,
                 scalar2=HS_EDGE,
                 op0=ALU.max,
                 op1=ALU.min,
             )
 
-        def abs_az(rows):
-            nc.scalar.activation(out=t_sb[:, rows, :], in_=az_sb[:, rows, :], func=ACT.Abs)
+        def abs_az(rows, cols=slice(0, U)):
+            nc.scalar.activation(out=t_sb[:, rows, cols], in_=az_sb[:, rows, cols], func=ACT.Abs)
 
-        def times_grad(rows):
+        def times_grad(rows, cols=slice(0, U)):
             nc.vector.scalar_tensor_tensor(
-                out=q5_sb[:, rows, :],
-                in0=q5_sb[:, rows, :],
+                out=q5_sb[:, rows, cols],
+                in0=q5_sb[:, rows, cols],
                 scalar=HS_EDGE,
-                in1=g_sb[:, rows, :],
+                in1=g_sb[:, rows, cols],
                 op0=ALU.subtract,
                 op1=ALU.mult,
             )
@@ -233,9 +235,11 @@ def tile_gruskipcell_v_kernel(
         ALL = slice(0, PACK)
         Z_COLS, R_COLS = slice(0, U), slice(U, 2 * U)
 
-        load(az_sb, a_zr, rows_of[0], Z_COLS)
-        load(g_sb, grad_out, row_pairs[0])
+        load(az_sb, a_zr, rows_of[0], col_halves[0], col_halves[0])
+        load(g_sb, grad_out, rows_of[0])
+        load(az_sb, a_zr, rows_of[0], col_halves[1], col_halves[1])
         load(az_sb, a_zr, rows_of[1], Z_COLS)
+        load(g_sb, grad_out, rows_of[1])
         load(az_sb, a_zr, rows_of[2], Z_COLS)
         load(g_sb, grad_out, row_pairs[1])
         load(az_sb, a_zr, rows_of[3], Z_COLS)
@@ -246,18 +250,23 @@ def tile_gruskipcell_v_kernel(
         load(ar_sb, a_zr, ALL, R_COLS)
         load(rh_sb, rec_h, ALL)
 
-        for j in range(PACK):
+        abs_az(rows_of[0], col_halves[0])
+        abs_az(rows_of[0], col_halves[1])
+        for j in range(1, PACK):
             abs_az(rows_of[j])
-        clip_az(rows_of[0])
-        times_grad(rows_of[0])
+        clip_az(rows_of[0], col_halves[0])
+        times_grad(rows_of[0], col_halves[0])
+        clip_az(rows_of[0], col_halves[1])
+        times_grad(rows_of[0], col_halves[1])
         clip_az(rows_of[1])
-        clip_az(rows_of[2])
+        masked_grad(rows_of[0])
         times_grad(rows_of[1])
+        clip_az(rows_of[2])
+        masked_grad(rows_of[1])
         times_grad(rows_of[2])
         clip_az(rows_of[3])
-        masked_grad(rows_of[0])
+        masked_grad(rows_of[2])
         times_grad(rows_of[3])
-        masked_grad(rows_of[1])
         square_hh(row_pairs[0])
         square_hh(row_pairs[1])
         regroup_x(0)
@@ -273,7 +282,7 @@ def tile_gruskipcell_v_kernel(
         b_codes = quantise(d_ah1)
         passes(a_codes, AH, (4, 5, 6, 7))
         abs_ar(ALL, col_halves[0])
-        masked_grad(row_pairs[1])
+        masked_grad(rows_of[3])
         for piece, cols in pieces_of_half(0):
             difference(ALL, cols)
         passes(b_codes, AH + N_TILE, (0, 1, 2, 3, 4, 5, 6, 7))
@@ -292,5 +301,5 @@ def tile_gruskipcell_v_kernel(
         d_ar1 = product_ar(1)
         passes(e_codes, AR, (0, 1, 2, 3))
         f_codes = quantise(d_ar1)
-        passes(e_codes, AR, (4, 5, 6, 7), (5, 7))
+        passes(e_codes, AR, (4, 5, 6, 7), (4, 5, 7))
         passes(f_codes, AR + N_TILE, (0, 1, 2, 3, 4, 5, 6, 7), (1, 3, 5, 7))

@@ -164,16 +164,15 @@ def tile_gruskipcell_v_kernel(
                 in_=x_grouped[:, cols, :].rearrange("p w j -> p (w j)"),
             )
 
-        def times_one_minus_square(rows):
-            for cols in col_halves:
-                nc.vector.scalar_tensor_tensor(
-                    out=q5_sb[:, rows, cols],
-                    in0=sq_sb[:, rows, cols],
-                    scalar=1.0,
-                    in1=q5_sb[:, rows, cols],
-                    op0=ALU.subtract,
-                    op1=ALU.mult,
-                )
+        def times_one_minus_square(rows, cols=slice(0, U)):
+            nc.vector.scalar_tensor_tensor(
+                out=q5_sb[:, rows, cols],
+                in0=sq_sb[:, rows, cols],
+                scalar=1.0,
+                in1=q5_sb[:, rows, cols],
+                op0=ALU.subtract,
+                op1=ALU.mult,
+            )
 
         def new_grouped():
             grouped = grouped_pool.tile([P, N_TILE, PACK], BF16, tag="grouped", align_bytes=64)
@@ -194,42 +193,41 @@ def tile_gruskipcell_v_kernel(
         def abs_ar(rows, cols):
             nc.scalar.activation(out=ar_sb[:, rows, cols], in_=ar_sb[:, rows, cols], func=ACT.Abs)
 
-        def product_az(c):
-            d_az = new_grouped()
-            for piece, cols in pieces_of_half(c):
-                nc.vector.scalar_tensor_tensor(
-                    out=d_az[:, piece, :],
-                    in0=token_last(t_sb[:, :, cols]),
-                    scalar=HS_SLOPE,
-                    in1=token_last(gm_sb[:, :, cols]),
-                    op0=ALU.mult,
-                    op1=ALU.mult,
-                )
-            return d_az
+        def product_az(d_az, c, k):
+            piece, cols = pieces_of_half(c)[k]
+            nc.vector.scalar_tensor_tensor(
+                out=d_az[:, piece, :],
+                in0=token_last(t_sb[:, :, cols]),
+                scalar=HS_SLOPE,
+                in1=token_last(gm_sb[:, :, cols]),
+                op0=ALU.mult,
+                op1=ALU.mult,
+            )
 
-        def masked_rec(c):
-            for piece, cols in pieces_of_half(c):
-                nc.vector.scalar_tensor_tensor(
-                    out=rh_sb[:, :, cols],
-                    in0=ar_sb[:, :, cols],
-                    scalar=HS_EDGE,
-                    in1=rh_sb[:, :, cols],
-                    op0=ALU.is_lt,
-                    op1=ALU.mult,
-                )
 
-        def product_ar(c):
-            d_ar = new_grouped()
-            for piece, cols in pieces_of_half(c):
-                nc.vector.scalar_tensor_tensor(
-                    out=d_ar[:, piece, :],
-                    in0=token_last(rh_sb[:, :, cols]),
-                    scalar=HS_SLOPE * HS_SLOPE,
-                    in1=token_last(q5_sb[:, :, cols]),
-                    op0=ALU.mult,
-                    op1=ALU.mult,
-                )
-            return d_ar
+        def masked_rec(c, k):
+            piece, cols = pieces_of_half(c)[k]
+            nc.vector.scalar_tensor_tensor(
+                out=rh_sb[:, :, cols],
+                in0=ar_sb[:, :, cols],
+                scalar=HS_EDGE,
+                in1=rh_sb[:, :, cols],
+                op0=ALU.is_lt,
+                op1=ALU.mult,
+            )
+
+
+        def product_ar(d_ar, c, k):
+            piece, cols = pieces_of_half(c)[k]
+            nc.vector.scalar_tensor_tensor(
+                out=d_ar[:, piece, :],
+                in0=token_last(rh_sb[:, :, cols]),
+                scalar=HS_SLOPE * HS_SLOPE,
+                in1=token_last(q5_sb[:, :, cols]),
+                op0=ALU.mult,
+                op1=ALU.mult,
+            )
+
 
         AH, AZ, AR = 2 * U, 0, U
         ALL = slice(0, PACK)
@@ -243,8 +241,8 @@ def tile_gruskipcell_v_kernel(
         load(az_sb, a_zr, rows_of[2], Z_COLS)
         load(g_sb, grad_out, row_pairs[1])
         load(az_sb, a_zr, rows_of[3], Z_COLS)
-        load(hh_sb, hh, row_pairs[0])
-        load(hh_sb, hh, row_pairs[1])
+        for j in range(PACK):
+            load(hh_sb, hh, rows_of[j])
         load(x_sb, inputs, ALL)
         load(h_sb, h_tm1, ALL)
         load(ar_sb, a_zr, ALL, R_COLS)
@@ -267,14 +265,16 @@ def tile_gruskipcell_v_kernel(
         clip_az(rows_of[3])
         masked_grad(rows_of[2])
         times_grad(rows_of[3])
-        square_hh(row_pairs[0])
-        square_hh(row_pairs[1])
+        for j in range(PACK):
+            square_hh(rows_of[j])
         regroup_x(0)
         regroup_x(1)
-        times_one_minus_square(row_pairs[0])
-        times_one_minus_square(row_pairs[1])
-        quantise_x(0)
+        for j in range(PACK - 1):
+            times_one_minus_square(rows_of[j])
+        for cols in col_halves:
+            times_one_minus_square(rows_of[PACK - 1], cols)
         d_ah0 = round_ah(0)
+        quantise_x(0)
         a_codes = quantise(d_ah0)
         passes(a_codes, AH, (0, 1, 2, 3))
         d_ah1 = round_ah(1)
@@ -283,22 +283,33 @@ def tile_gruskipcell_v_kernel(
         passes(a_codes, AH, (4, 5, 6, 7))
         abs_ar(ALL, col_halves[0])
         masked_grad(rows_of[3])
-        for piece, cols in pieces_of_half(0):
-            difference(ALL, cols)
+        difference(ALL, pieces_of_half(0)[0][1])
+        difference(ALL, pieces_of_half(0)[1][1])
         passes(b_codes, AH + N_TILE, (0, 1, 2, 3, 4, 5, 6, 7))
-        d_az0 = product_az(0)
-        difference(ALL, col_halves[1])
+        d_az0 = new_grouped()
+        product_az(d_az0, 0, 0)
+        product_az(d_az0, 0, 1)
         c_codes = quantise(d_az0)
         abs_ar(ALL, col_halves[1])
-        d_az1 = product_az(1)
+        difference(ALL, pieces_of_half(1)[0][1])
+        difference(ALL, pieces_of_half(1)[1][1])
+        d_az1 = new_grouped()
+        product_az(d_az1, 1, 0)
+        product_az(d_az1, 1, 1)
         passes(c_codes, AZ, (0, 1, 2, 3, 4, 5, 6, 7))
-        masked_rec(0)
         d_codes = quantise(d_az1)
-        masked_rec(1)
-        d_ar0 = product_ar(0)
+        masked_rec(0, 0)
+        masked_rec(0, 1)
+        d_ar0 = new_grouped()
+        product_ar(d_ar0, 0, 0)
+        product_ar(d_ar0, 0, 1)
         passes(d_codes, AZ + N_TILE, (0, 1, 2, 3, 4, 5, 6, 7))
         e_codes = quantise(d_ar0)
-        d_ar1 = product_ar(1)
+        masked_rec(1, 0)
+        masked_rec(1, 1)
+        d_ar1 = new_grouped()
+        product_ar(d_ar1, 1, 0)
+        product_ar(d_ar1, 1, 1)
         passes(e_codes, AR, (0, 1, 2, 3))
         f_codes = quantise(d_ar1)
         passes(e_codes, AR, (4, 5, 6, 7), (4, 5, 7))

@@ -109,13 +109,8 @@ def tile_gruskipcell_v_kernel(
                 nc.sync.dma_start(out=out[m_cols, first_column : first_column + N_TILE], in_=staged[:])
 
         def clip_az(rows, cols=slice(0, U)):
-            nc.vector.tensor_scalar(
-                out=q5_sb[:, rows, cols],
-                in0=az_sb[:, rows, cols],
-                scalar1=-HS_EDGE,
-                scalar2=HS_EDGE,
-                op0=ALU.max,
-                op1=ALU.min,
+            nc.scalar.activation(
+                out=q5_sb[:, rows, cols], in_=az_sb[:, rows, cols], func=ACT.Relu, scale=-1.0, bias=HS_EDGE
             )
 
         def abs_az(rows, cols=slice(0, U)):
@@ -125,9 +120,9 @@ def tile_gruskipcell_v_kernel(
             nc.vector.scalar_tensor_tensor(
                 out=q5_sb[:, rows, cols],
                 in0=q5_sb[:, rows, cols],
-                scalar=HS_EDGE,
+                scalar=2.0 * HS_EDGE,
                 in1=g_sb[:, rows, cols],
-                op0=ALU.subtract,
+                op0=ALU.min,
                 op1=ALU.mult,
             )
 
@@ -184,7 +179,7 @@ def tile_gruskipcell_v_kernel(
                 nc.vector.tensor_scalar(
                     out=d_ah[:, piece, :],
                     in0=token_last(q5_sb[:, :, cols]),
-                    scalar1=HS_SLOPE,
+                    scalar1=-HS_SLOPE,
                     scalar2=None,
                     op0=ALU.mult,
                 )
@@ -222,7 +217,7 @@ def tile_gruskipcell_v_kernel(
             nc.vector.scalar_tensor_tensor(
                 out=d_ar[:, piece, :],
                 in0=token_last(rh_sb[:, :, cols]),
-                scalar=HS_SLOPE * HS_SLOPE,
+                scalar=-HS_SLOPE * HS_SLOPE,
                 in1=token_last(q5_sb[:, :, cols]),
                 op0=ALU.mult,
                 op1=ALU.mult,
@@ -248,23 +243,22 @@ def tile_gruskipcell_v_kernel(
         load(ar_sb, a_zr, ALL, R_COLS)
         load(rh_sb, rec_h, ALL)
 
+        clip_az(rows_of[0], col_halves[0])
         abs_az(rows_of[0], col_halves[0])
+        clip_az(rows_of[0], col_halves[1])
         abs_az(rows_of[0], col_halves[1])
         for j in range(1, PACK):
+            clip_az(rows_of[j])
             abs_az(rows_of[j])
-        clip_az(rows_of[0], col_halves[0])
         times_grad(rows_of[0], col_halves[0])
-        clip_az(rows_of[0], col_halves[1])
         times_grad(rows_of[0], col_halves[1])
-        clip_az(rows_of[1])
         masked_grad(rows_of[0])
         times_grad(rows_of[1])
-        clip_az(rows_of[2])
         masked_grad(rows_of[1])
         times_grad(rows_of[2])
-        clip_az(rows_of[3])
         masked_grad(rows_of[2])
         times_grad(rows_of[3])
+        masked_grad(rows_of[3])
         for j in range(PACK):
             square_hh(rows_of[j])
         regroup_x(0)
@@ -282,7 +276,6 @@ def tile_gruskipcell_v_kernel(
         b_codes = quantise(d_ah1)
         passes(a_codes, AH, (4, 5, 6, 7))
         abs_ar(ALL, col_halves[0])
-        masked_grad(rows_of[3])
         difference(ALL, pieces_of_half(0)[0][1])
         difference(ALL, pieces_of_half(0)[1][1])
         passes(b_codes, AH + N_TILE, (0, 1, 2, 3, 4, 5, 6, 7))
@@ -310,7 +303,7 @@ def tile_gruskipcell_v_kernel(
         d_ar1 = new_grouped()
         product_ar(d_ar1, 1, 0)
         product_ar(d_ar1, 1, 1)
-        passes(e_codes, AR, (0, 1, 2, 3))
+        passes(e_codes, AR, (0, 1))
         f_codes = quantise(d_ar1)
-        passes(e_codes, AR, (4, 5, 6, 7), (4, 5, 7))
-        passes(f_codes, AR + N_TILE, (0, 1, 2, 3, 4, 5, 6, 7), (1, 3, 5, 7))
+        passes(e_codes, AR, (2, 3, 4, 5, 6, 7), (2, 4, 5, 7))
+        passes(f_codes, AR + N_TILE, (0, 1, 2, 3, 4, 5, 6, 7), (0, 2, 4, 6))

@@ -305,5 +305,5 @@ def tile_gruskipcell_v_kernel(
         product_ar(d_ar1, 1, 1)
         passes(e_codes, AR, (0, 1))
         f_codes = quantise(d_ar1)
-        passes(e_codes, AR, (2, 3, 4, 5, 6, 7), (2, 4, 5, 7))
+        passes(e_codes, AR, (2, 3, 4, 5, 6, 7))
         passes(f_codes, AR + N_TILE, (0, 1, 2, 3, 4, 5, 6, 7), (0, 2, 4, 6))

@@ -4,6 +4,7 @@ F32 = mybir.dt.float32
 BF16 = mybir.dt.bfloat16
 U32 = mybir.dt.uint32
 U8 = mybir.dt.uint8
+I32 = mybir.dt.int32
 E4M3X4 = mybir.dt.float8_e4m3fn_x4
 E5M2X4 = mybir.dt.float8_e5m2_x4
 ALU = mybir.AluOpType
@@ -21,6 +22,7 @@ HALVES = U // N_TILE
 PIECE = N_TILE // 2
 HS_SLOPE = 0.2
 HS_EDGE = 2.5
+ALL_BUT_SIGN = 0x7FFFFFFF
 
 FLOPS = 2 * TOKENS * D * 3 * U
 BYTES = 2 * TOKENS * (D + 2 * U) + 4 * TOKENS * 4 * U + 4 * D * 3 * U
@@ -76,15 +78,17 @@ def tile_gruskipcell_v_kernel(
             else:
                 nc.sync.dma_start(out=tile[:, rows, to_cols], in_=by_partition(dram)[:, rows, cols])
 
-        def quantise(grouped):
+        def quantise(grouped, after_piece=None):
             dm_codes = quantised.tile([P, N_TILE], U32, align_bytes=64)
             dm_scales = quantised.tile([P, N_TILE], U8, align_bytes=64)
-            for piece in pieces:
+            for k, piece in enumerate(pieces):
                 nc.vector.quantize_mx(
                     out=dm_codes[:, piece].bitcast(E5M2X4),
                     scales=dm_scales[:, piece],
                     in_=grouped[:, piece, :].rearrange("p w j -> p (w j)"),
                 )
+                if after_piece is not None:
+                    after_piece(k)
             return dm_codes, dm_scales
 
         def passes(codes, first_column, ms, vector_ms=()):
@@ -185,8 +189,12 @@ def tile_gruskipcell_v_kernel(
                 )
             return d_ah
 
-        def abs_ar(rows, cols):
-            nc.scalar.activation(out=ar_sb[:, rows, cols], in_=ar_sb[:, rows, cols], func=ACT.Abs)
+        def abs_ar(c, k):
+            cols = pieces_of_half(c)[k][1]
+            bits = ar_sb[:, :, cols].bitcast(I32)
+            nc.vector.tensor_scalar(
+                out=bits, in0=bits, scalar1=ALL_BUT_SIGN, scalar2=None, op0=ALU.bitwise_and
+            )
 
         def product_az(d_az, c, k):
             piece, cols = pieces_of_half(c)[k]
@@ -275,7 +283,6 @@ def tile_gruskipcell_v_kernel(
         quantise_x(1)
         b_codes = quantise(d_ah1)
         passes(a_codes, AH, (4, 5, 6, 7))
-        abs_ar(ALL, col_halves[0])
         difference(ALL, pieces_of_half(0)[0][1])
         difference(ALL, pieces_of_half(0)[1][1])
         passes(b_codes, AH + N_TILE, (0, 1, 2, 3, 4, 5, 6, 7))
@@ -283,21 +290,20 @@ def tile_gruskipcell_v_kernel(
         product_az(d_az0, 0, 0)
         product_az(d_az0, 0, 1)
         c_codes = quantise(d_az0)
-        abs_ar(ALL, col_halves[1])
         difference(ALL, pieces_of_half(1)[0][1])
         difference(ALL, pieces_of_half(1)[1][1])
         d_az1 = new_grouped()
         product_az(d_az1, 1, 0)
         product_az(d_az1, 1, 1)
         passes(c_codes, AZ, (0, 1, 2, 3, 4, 5, 6, 7))
-        d_codes = quantise(d_az1)
+        d_codes = quantise(d_az1, lambda k: abs_ar(0, k))
         masked_rec(0, 0)
         masked_rec(0, 1)
         d_ar0 = new_grouped()
         product_ar(d_ar0, 0, 0)
         product_ar(d_ar0, 0, 1)
         passes(d_codes, AZ + N_TILE, (0, 1, 2, 3, 4, 5, 6, 7))
-        e_codes = quantise(d_ar0)
+        e_codes = quantise(d_ar0, lambda k: abs_ar(1, k))
         masked_rec(1, 0)
         masked_rec(1, 1)
         d_ar1 = new_grouped()

@@ -189,6 +189,9 @@ def tile_gruskipcell_v_kernel(
                 )
             return d_ah
 
+        def scalar_abs_ar(rows, cols):
+            nc.scalar.activation(out=ar_sb[:, rows, cols], in_=ar_sb[:, rows, cols], func=ACT.Abs)
+
         def abs_ar(c, k):
             cols = pieces_of_half(c)[k][1]
             bits = ar_sb[:, :, cols].bitcast(I32)
@@ -296,6 +299,7 @@ def tile_gruskipcell_v_kernel(
         product_az(d_az1, 1, 0)
         product_az(d_az1, 1, 1)
         passes(c_codes, AZ, (0, 1, 2, 3, 4, 5, 6, 7))
+        scalar_abs_ar(ALL, col_halves[1])
         d_codes = quantise(d_az1, lambda k: abs_ar(0, k))
         masked_rec(0, 0)
         masked_rec(0, 1)
@@ -303,7 +307,7 @@ def tile_gruskipcell_v_kernel(
         product_ar(d_ar0, 0, 0)
         product_ar(d_ar0, 0, 1)
         passes(d_codes, AZ + N_TILE, (0, 1, 2, 3, 4, 5, 6, 7))
-        e_codes = quantise(d_ar0, lambda k: abs_ar(1, k))
+        e_codes = quantise(d_ar0)
         masked_rec(1, 0)
         masked_rec(1, 1)
         d_ar1 = new_grouped()

@@ -53,8 +53,8 @@ def tile_gruskipcell_v_kernel(
     with tc.tile_pool(name="resident", bufs=1) as resident, tc.tile_pool(
         name="grouped", bufs=3
     ) as grouped_pool, tc.tile_pool(name="quantised", bufs=3) as quantised, tc.tile_pool(
-        name="staging", bufs=16
-    ) as staging, tc.psum_pool(name="banks", bufs=8) as banks, tc.manual_schedule():
+        name="staging", bufs=14
+    ) as staging, tc.tile_pool(name="wide_staging", bufs=9) as wide_staging, tc.psum_pool(name="banks", bufs=8) as banks, tc.manual_schedule():
         x_sb = resident.tile([P, PACK, D], BF16)
         g_sb = resident.tile([P, PACK, U], BF16)
         h_sb = resident.tile([P, PACK, U], BF16)
@@ -65,7 +65,6 @@ def tile_gruskipcell_v_kernel(
         q5_sb = resident.tile([P, PACK, U], F32)
         gm_sb = resident.tile([P, PACK, U], BF16)
         t_sb = resident.tile([P, PACK, U], F32)
-        sq_sb = resident.tile([P, PACK, U], F32)
         x_grouped = resident.tile([P, D, PACK], BF16, align_bytes=64)
         x_codes = resident.tile([P, D], U32, align_bytes=64)
         x_scales = resident.tile([P, D], U8, align_bytes=64)
@@ -90,6 +89,24 @@ def tile_gruskipcell_v_kernel(
                 if after_piece is not None:
                     after_piece(k)
             return dm_codes, dm_scales
+
+        def wide_passes(first_codes, second_codes, first_column, ms):
+            for m in ms:
+                m_cols = slice(m * M_TILE, (m + 1) * M_TILE)
+                staged = wide_staging.tile([P, U], F32)
+                for cols, (dm_codes, dm_scales) in zip(col_halves, (first_codes, second_codes)):
+                    acc = banks.tile([P, N_TILE], F32)
+                    nc.tensor.matmul_mx(
+                        out=acc[:],
+                        lhsT=x_codes[:, m_cols].bitcast(E4M3X4),
+                        lhsT_scale=x_scales[:, m_cols],
+                        rhs=dm_codes[:].bitcast(E5M2X4),
+                        rhs_scale=dm_scales[:],
+                        start=True,
+                        stop=True,
+                    )
+                    nc.scalar.copy(out=staged[:, cols], in_=acc[:])
+                nc.sync.dma_start(out=out[m_cols, first_column : first_column + U], in_=staged[:])
 
         def passes(codes, first_column, ms, vector_ms=()):
             dm_codes, dm_scales = codes
@@ -141,7 +158,7 @@ def tile_gruskipcell_v_kernel(
             )
 
         def square_hh(rows):
-            nc.scalar.activation(out=sq_sb[:, rows, :], in_=hh_sb[:, rows, :], func=ACT.Square)
+            nc.scalar.activation(out=az_sb[:, rows, :], in_=hh_sb[:, rows, :], func=ACT.Square)
 
         def difference(rows, cols):
             nc.vector.tensor_tensor(
@@ -166,7 +183,7 @@ def tile_gruskipcell_v_kernel(
         def times_one_minus_square(rows, cols=slice(0, U)):
             nc.vector.scalar_tensor_tensor(
                 out=q5_sb[:, rows, cols],
-                in0=sq_sb[:, rows, cols],
+                in0=az_sb[:, rows, cols],
                 scalar=1.0,
                 in1=q5_sb[:, rows, cols],
                 op0=ALU.subtract,
@@ -285,10 +302,10 @@ def tile_gruskipcell_v_kernel(
         d_ah1 = round_ah(1)
         quantise_x(1)
         b_codes = quantise(d_ah1)
-        passes(a_codes, AH, (4, 5, 6, 7))
+        wide_passes(a_codes, b_codes, AH, (4, 5, 6, 7))
         difference(ALL, pieces_of_half(0)[0][1])
         difference(ALL, pieces_of_half(0)[1][1])
-        passes(b_codes, AH + N_TILE, (0, 1, 2, 3, 4, 5, 6, 7))
+        passes(b_codes, AH + N_TILE, (0, 1, 2, 3))
         d_az0 = new_grouped()
         product_az(d_az0, 0, 0)
         product_az(d_az0, 0, 1)
@@ -298,7 +315,7 @@ def tile_gruskipcell_v_kernel(
         d_az1 = new_grouped()
         product_az(d_az1, 1, 0)
         product_az(d_az1, 1, 1)
-        passes(c_codes, AZ, (0, 1, 2, 3, 4, 5, 6, 7))
+        passes(c_codes, AZ, (0, 1, 2, 3))
         scalar_abs_ar(ALL, col_halves[1])
         d_codes = quantise(d_az1, lambda k: abs_ar(0, k))
         masked_rec(0, 0)
@@ -306,7 +323,8 @@ def tile_gruskipcell_v_kernel(
         d_ar0 = new_grouped()
         product_ar(d_ar0, 0, 0)
         product_ar(d_ar0, 0, 1)
-        passes(d_codes, AZ + N_TILE, (0, 1, 2, 3, 4, 5, 6, 7))
+        wide_passes(c_codes, d_codes, AZ, (4, 5, 6, 7))
+        passes(d_codes, AZ + N_TILE, (0, 1, 2, 3))
         e_codes = quantise(d_ar0)
         masked_rec(1, 0)
         masked_rec(1, 1)

import concourse.mybir as mybir

F32 = mybir.dt.float32
BF16 = mybir.dt.bfloat16
U32 = mybir.dt.uint32
U8 = mybir.dt.uint8
I32 = mybir.dt.int32
E4M3X4 = mybir.dt.float8_e4m3fn_x4
E5M2X4 = mybir.dt.float8_e5m2_x4
ALU = mybir.AluOpType
ACT = mybir.ActivationFunctionType

P = 128
PACK = 4
TOKENS = P * PACK
D = 1024
U = 1024
M_TILE = 128
N_TILE = 512
M_TILES = D // M_TILE
HALVES = U // N_TILE
PIECE = N_TILE // 2
HS_SLOPE = 0.2
HS_EDGE = 2.5
ALL_BUT_SIGN = 0x7FFFFFFF

FLOPS = 2 * TOKENS * D * 3 * U
BYTES = 2 * TOKENS * (D + 2 * U) + 4 * TOKENS * 4 * U + 4 * D * 3 * U


def tile_gruskipcell_v_kernel(
    tc, inputs, h_tm1, kernel, recurrent_kernel, bias, a_zr, rec_h, hh, grad_out, out
):
    nc = tc.nc

    def by_partition(dram):
        return dram.rearrange("(p j) w -> p j w", j=PACK)

    def token_last(tile_ap):
        return tile_ap.rearrange("p j w -> p w j")

    rows_of = [slice(j, j + 1) for j in range(PACK)]
    row_pairs = [slice(0, 2), slice(2, 4)]
    col_halves = [slice(c * N_TILE, (c + 1) * N_TILE) for c in range(HALVES)]
    pieces = [slice(k * PIECE, (k + 1) * PIECE) for k in range(N_TILE // PIECE)]

    def pieces_of_half(c):
        return [
            (pieces[k], slice(c * N_TILE + k * PIECE, c * N_TILE + (k + 1) * PIECE))
            for k in range(N_TILE // PIECE)
        ]

    with tc.tile_pool(name="resident", bufs=1) as resident, tc.tile_pool(
        name="grouped", bufs=3
    ) as grouped_pool, tc.tile_pool(name="quantised", bufs=3) as quantised, tc.tile_pool(
        name="staging", bufs=14
    ) as staging, tc.tile_pool(name="wide_staging", bufs=9) as wide_staging, tc.psum_pool(name="banks", bufs=8) as banks, tc.manual_schedule():
        x_sb = resident.tile([P, PACK, D], BF16)
        g_sb = resident.tile([P, PACK, U], BF16)
        h_sb = resident.tile([P, PACK, U], BF16)
        az_sb = resident.tile([P, PACK, U], F32)
        hh_sb = resident.tile([P, PACK, U], F32)
        ar_sb = resident.tile([P, PACK, U], F32)
        rh_sb = resident.tile([P, PACK, U], F32)
        q5_sb = resident.tile([P, PACK, U], F32)
        gm_sb = resident.tile([P, PACK, U], BF16)
        t_sb = resident.tile([P, PACK, U], F32)
        x_grouped = resident.tile([P, D, PACK], BF16, align_bytes=64)
        x_codes = resident.tile([P, D], U32, align_bytes=64)
        x_scales = resident.tile([P, D], U8, align_bytes=64)

        def load(tile, dram, rows, cols=None, to_cols=None):
            if cols is None:
                nc.sync.dma_start(out=tile[:, rows, :], in_=by_partition(dram)[:, rows, :])
            elif to_cols is None:
                nc.sync.dma_start(out=tile[:, rows, :], in_=by_partition(dram)[:, rows, cols])
            else:
                nc.sync.dma_start(out=tile[:, rows, to_cols], in_=by_partition(dram)[:, rows, cols])

        def quantise(grouped, after_piece=None):
            dm_codes = quantised.tile([P, N_TILE], U32, align_bytes=64)
            dm_scales = quantised.tile([P, N_TILE], U8, align_bytes=64)
            for k, piece in enumerate(pieces):
                nc.vector.quantize_mx(
                    out=dm_codes[:, piece].bitcast(E5M2X4),
                    scales=dm_scales[:, piece],
                    in_=grouped[:, piece, :].rearrange("p w j -> p (w j)"),
                )
                if after_piece is not None:
                    after_piece(k)
            return dm_codes, dm_scales

        def wide_passes(first_codes, second_codes, first_column, ms):
            for m in ms:
                m_cols = slice(m * M_TILE, (m + 1) * M_TILE)
                staged = wide_staging.tile([P, U], F32)
                for cols, (dm_codes, dm_scales) in zip(col_halves, (first_codes, second_codes)):
                    acc = banks.tile([P, N_TILE], F32)
                    nc.tensor.matmul_mx(
                        out=acc[:],
                        lhsT=x_codes[:, m_cols].bitcast(E4M3X4),
                        lhsT_scale=x_scales[:, m_cols],
                        rhs=dm_codes[:].bitcast(E5M2X4),
                        rhs_scale=dm_scales[:],
                        start=True,
                        stop=True,
                    )
                    nc.scalar.copy(out=staged[:, cols], in_=acc[:])
                nc.sync.dma_start(out=out[m_cols, first_column : first_column + U], in_=staged[:])

        def passes(codes, first_column, ms, vector_ms=()):
            dm_codes, dm_scales = codes
            for m in ms:
                m_cols = slice(m * M_TILE, (m + 1) * M_TILE)
                acc = banks.tile([P, N_TILE], F32)
                nc.tensor.matmul_mx(
                    out=acc[:],
                    lhsT=x_codes[:, m_cols].bitcast(E4M3X4),
                    lhsT_scale=x_scales[:, m_cols],
                    rhs=dm_codes[:].bitcast(E5M2X4),
                    rhs_scale=dm_scales[:],
                    start=True,
                    stop=True,
                )
                staged = staging.tile([P, N_TILE], F32)
                if m in vector_ms:
                    nc.vector.tensor_copy(out=staged[:], in_=acc[:])
                else:
                    nc.scalar.copy(out=staged[:], in_=acc[:])
                nc.sync.dma_start(out=out[m_cols, first_column : first_column + N_TILE], in_=staged[:])

        def clip_az(rows, cols=slice(0, U)):
            nc.scalar.activation(
                out=q5_sb[:, rows, cols], in_=az_sb[:, rows, cols], func=ACT.Relu, scale=-1.0, bias=HS_EDGE
            )

        def abs_az(rows, cols=slice(0, U)):
            nc.scalar.activation(out=t_sb[:, rows, cols], in_=az_sb[:, rows, cols], func=ACT.Abs)

        def times_grad(rows, cols=slice(0, U)):
            nc.vector.scalar_tensor_tensor(
                out=q5_sb[:, rows, cols],
                in0=q5_sb[:, rows, cols],
                scalar=2.0 * HS_EDGE,
                in1=g_sb[:, rows, cols],
                op0=ALU.min,
                op1=ALU.mult,
            )

        def masked_grad(rows):
            nc.vector.scalar_tensor_tensor(
                out=gm_sb[:, rows, :],
                in0=t_sb[:, rows, :],
                scalar=HS_EDGE,
                in1=g_sb[:, rows, :],
                op0=ALU.is_lt,
                op1=ALU.mult,
            )

        def square_hh(rows):
            nc.scalar.activation(out=az_sb[:, rows, :], in_=hh_sb[:, rows, :], func=ACT.Square)

        def difference(rows, cols):
            nc.vector.tensor_tensor(
                out=t_sb[:, rows, cols], in0=h_sb[:, rows, cols], in1=hh_sb[:, rows, cols], op=ALU.subtract
            )

        def regroup_x(c):
            cols = col_halves[c]
            nc.scalar.copy(
                out=x_grouped[:, cols, :].rearrange("p (c i) j -> p c j i", i=4),
                in_=x_sb[:, :, cols].rearrange("p j (c i) -> p c j i", i=4),
            )

        def quantise_x(c):
            cols = col_halves[c]
            nc.vector.quantize_mx(
                out=x_codes[:, cols].bitcast(E4M3X4),
                scales=x_scales[:, cols],
                in_=x_grouped[:, cols, :].rearrange("p w j -> p (w j)"),
            )

        def times_one_minus_square(rows, cols=slice(0, U)):
            nc.vector.scalar_tensor_tensor(
                out=q5_sb[:, rows, cols],
                in0=az_sb[:, rows, cols],
                scalar=1.0,
                in1=q5_sb[:, rows, cols],
                op0=ALU.subtract,
                op1=ALU.mult,
            )

        def new_grouped():
            grouped = grouped_pool.tile([P, N_TILE, PACK], BF16, tag="grouped", align_bytes=64)
            return grouped

        def round_ah(c):
            d_ah = new_grouped()
            for piece, cols in pieces_of_half(c):
                nc.vector.tensor_scalar(
                    out=d_ah[:, piece, :],
                    in0=token_last(q5_sb[:, :, cols]),
                    scalar1=-HS_SLOPE,
                    scalar2=None,
                    op0=ALU.mult,
                )
            return d_ah

        def scalar_abs_ar(rows, cols):
            nc.scalar.activation(out=ar_sb[:, rows, cols], in_=ar_sb[:, rows, cols], func=ACT.Abs)

        def abs_ar(c, k):
            cols = pieces_of_half(c)[k][1]
            bits = ar_sb[:, :, cols].bitcast(I32)
            nc.vector.tensor_scalar(
                out=bits, in0=bits, scalar1=ALL_BUT_SIGN, scalar2=None, op0=ALU.bitwise_and
            )

        def product_az(d_az, c, k):
            piece, cols = pieces_of_half(c)[k]
            nc.vector.scalar_tensor_tensor(
                out=d_az[:, piece, :],
                in0=token_last(t_sb[:, :, cols]),
                scalar=HS_SLOPE,
                in1=token_last(gm_sb[:, :, cols]),
                op0=ALU.mult,
                op1=ALU.mult,
            )


        def masked_rec(c, k):
            piece, cols = pieces_of_half(c)[k]
            nc.vector.scalar_tensor_tensor(
                out=rh_sb[:, :, cols],
                in0=ar_sb[:, :, cols],
                scalar=HS_EDGE,
                in1=rh_sb[:, :, cols],
                op0=ALU.is_lt,
                op1=ALU.mult,
            )


        def product_ar(d_ar, c, k):
            piece, cols = pieces_of_half(c)[k]
            nc.vector.scalar_tensor_tensor(
                out=d_ar[:, piece, :],
                in0=token_last(rh_sb[:, :, cols]),
                scalar=-HS_SLOPE * HS_SLOPE,
                in1=token_last(q5_sb[:, :, cols]),
                op0=ALU.mult,
                op1=ALU.mult,
            )


        AH, AZ, AR = 2 * U, 0, U
        ALL = slice(0, PACK)
        Z_COLS, R_COLS = slice(0, U), slice(U, 2 * U)

        load(az_sb, a_zr, rows_of[0], col_halves[0], col_halves[0])
        load(g_sb, grad_out, rows_of[0])
        load(az_sb, a_zr, rows_of[0], col_halves[1], col_halves[1])
        load(az_sb, a_zr, rows_of[1], Z_COLS)
        load(g_sb, grad_out, rows_of[1])
        load(az_sb, a_zr, rows_of[2], Z_COLS)
        load(g_sb, grad_out, row_pairs[1])
        load(az_sb, a_zr, rows_of[3], Z_COLS)
        for j in range(PACK):
            load(hh_sb, hh, rows_of[j])
        load(x_sb, inputs, ALL)
        load(h_sb, h_tm1, ALL)
        load(ar_sb, a_zr, ALL, R_COLS)
        load(rh_sb, rec_h, ALL)

        clip_az(rows_of[0], col_halves[0])
        abs_az(rows_of[0], col_halves[0])
        clip_az(rows_of[0], col_halves[1])
        abs_az(rows_of[0], col_halves[1])
        for j in range(1, PACK):
            clip_az(rows_of[j])
            abs_az(rows_of[j])
        times_grad(rows_of[0], col_halves[0])
        times_grad(rows_of[0], col_halves[1])
        masked_grad(rows_of[0])
        times_grad(rows_of[1])
        masked_grad(rows_of[1])
        times_grad(rows_of[2])
        masked_grad(rows_of[2])
        times_grad(rows_of[3])
        masked_grad(rows_of[3])
        for j in range(PACK):
            square_hh(rows_of[j])
        regroup_x(0)
        regroup_x(1)
        for j in range(PACK - 1):
            times_one_minus_square(rows_of[j])
        for cols in col_halves:
            times_one_minus_square(rows_of[PACK - 1], cols)
        d_ah0 = round_ah(0)
        quantise_x(0)
        a_codes = quantise(d_ah0)
        passes(a_codes, AH, (0, 1, 2, 3))
        d_ah1 = round_ah(1)
        quantise_x(1)
        b_codes = quantise(d_ah1)
        wide_passes(a_codes, b_codes, AH, (4, 5, 6, 7))
        difference(ALL, pieces_of_half(0)[0][1])
        difference(ALL, pieces_of_half(0)[1][1])
        passes(b_codes, AH + N_TILE, (0, 1, 2, 3))
        d_az0 = new_grouped()
        product_az(d_az0, 0, 0)
        product_az(d_az0, 0, 1)
        c_codes = quantise(d_az0)
        difference(ALL, pieces_of_half(1)[0][1])
        difference(ALL, pieces_of_half(1)[1][1])
        d_az1 = new_grouped()
        product_az(d_az1, 1, 0)
        product_az(d_az1, 1, 1)
        passes(c_codes, AZ, (0, 1, 2, 3))
        scalar_abs_ar(ALL, col_halves[1])
        d_codes = quantise(d_az1, lambda k: abs_ar(0, k))
        masked_rec(0, 0)
        masked_rec(0, 1)
        d_ar0 = new_grouped()
        product_ar(d_ar0, 0, 0)
        product_ar(d_ar0, 0, 1)
        wide_passes(c_codes, d_codes, AZ, (4, 5, 6, 7))
        passes(d_codes, AZ + N_TILE, (0, 1, 2, 3))
        e_codes = quantise(d_ar0)
        masked_rec(1, 0)
        masked_rec(1, 1)
        d_ar1 = new_grouped()
        product_ar(d_ar1, 1, 0)
        product_ar(d_ar1, 1, 1)
        passes(e_codes, AR, (0, 1))
        f_codes = quantise(d_ar1)
        passes(e_codes, AR, (2, 3, 4, 5, 6, 7))
        passes(f_codes, AR + N_TILE, (0, 1, 2, 3, 4, 5, 6, 7), (0, 2, 4, 6))
